import numpy as np
import ml_dtypes


def mxq(x, axis, fmt="e4m3"):
    dtype, down = {"e4m3": (ml_dtypes.float8_e4m3fn, 7), "e5m2": (ml_dtypes.float8_e5m2, 14)}[fmt]
    v = np.moveaxis(np.asarray(x, np.float32).astype(ml_dtypes.bfloat16).astype(np.float64), axis, -1)
    blocks = v.reshape(v.shape[:-1] + (-1, 32))
    amax = np.abs(blocks).max(-1, keepdims=True)
    byte = np.maximum(np.where(amax > 0, np.frexp(amax)[1] - 1 + 127, 0) - down, 1)
    scale = np.exp2(byte - 127.0)
    codes = (blocks / scale).astype(np.float32).astype(dtype).astype(np.float64)
    return np.moveaxis((codes * scale).reshape(v.shape), -1, axis)


WIDE = False


def mx_kscale(k):
    if not WIDE:
        return np.ones(k)
    levels = np.array([20, -20, 10, -10, 0])
    a = np.random.permutation(np.resize(levels, k // 512 * 4)).reshape(k // 512, 4)
    idx = np.arange(k)
    return np.exp2(a[idx // 512, idx % 128 // 32])


BF16 = ml_dtypes.bfloat16


def bf(x):
    return np.asarray(x, np.float32).astype(BF16)


def f64(x):
    return np.asarray(x).astype(np.float64)


B, N, D, H = 32, 16, 512, 1024
T = B * N * N


def hidden(xi_p, xj_p, mb1):
    return np.maximum(f64(xi_p)[:, :, None, :] + f64(xj_p)[:, None, :, :] + f64(mb1), 0.0)


def setup_inputs():
    c = mx_kscale(T).reshape(B, N * N)[:, 0][:, None, None]
    xi0 = bf(np.random.standard_normal((B, N, H)) * 0.7)
    xj0 = bf(np.random.standard_normal((B, N, H)) * 0.7)
    node_mask = bf(np.random.uniform(size=(B, N)) < 0.9)
    mb1 = bf(np.random.standard_normal(H) * 0.2)
    mw2 = bf(np.random.standard_normal((H, D)) * 0.5 / np.sqrt(H))
    mb2 = bf(np.random.standard_normal(D) * 0.1)
    g = bf(np.random.standard_normal((B, N, D)) * np.exp2(np.random.randint(-12, 1, (B, N, 1))) * 0.25 * c)
    z = hidden(xi0, xj0, mb1) @ f64(mw2) + f64(mb2)
    return {
        "xi_p": bf(f64(xi0) / c),
        "xj_p": bf(f64(xj0) / c),
        "node_mask": node_mask,
        "mb1": mb1,
        "mw2": mw2,
        "mb2": mb2,
        "z": np.asarray(z, np.float32),
        "grad_out": g,
    }


def reference(xi_p, xj_p, node_mask, mb1, mw2, mb2, z, grad_out):
    h = hidden(xi_p, xj_p, mb1).reshape(T, H)
    dz = f64(grad_out)[:, :, None, :] * f64(node_mask)[:, None, :, None] * (f64(z) > 0.0)
    dz = dz.reshape(T, D)
    return mxq(h, 0, "e4m3").T @ mxq(dz, 0, "e5m2")

@@ -1,0 +1,202 @@
+from contextlib import ExitStack
+
+import concourse.mybir as mybir
+
+F32 = mybir.dt.float32
+BF16 = mybir.dt.bfloat16
+U32 = mybir.dt.uint32
+U8 = mybir.dt.uint8
+E4M3_X4 = mybir.dt.float8_e4m3fn_x4
+E5M2_X4 = mybir.dt.float8_e5m2_x4
+ALU = mybir.AluOpType
+ACT = mybir.ActivationFunctionType
+
+P = 128
+PACK = 4
+GRAPHS, NODES, D_OUT, HID = 32, 16, 512, 1024
+BH = 2
+BL = GRAPHS // BH
+R = P // BL
+IL = NODES // R
+JQ = NODES // PACK
+K_TILES = HID // P
+
+FLOPS = 2 * GRAPHS * NODES * NODES * HID * D_OUT
+BYTES = (
+    GRAPHS * NODES * NODES * D_OUT * 4
+    + 2 * GRAPHS * NODES * HID * 2
+    + GRAPHS * NODES * D_OUT * 2
+    + GRAPHS * NODES * 2
+    + HID * 2
+    + HID * D_OUT * 4
+)
+
+
+H_HALVES = 2
+HALF = HID // H_HALVES
+N_PASS = BH * JQ * IL
+
+
+def tile_graphdynamics_pa_t_v_kernel(
+    tc, xi_p, xj_p, node_mask, mb1, mw2, mb2, z, grad_out, out
+):
+    nc = tc.nc
+
+    xi_rows = xi_p.rearrange("(bh bl) (r il) k -> bh (bl r) (il k)", bh=BH, il=IL)
+    g_rows = grad_out.rearrange("(bh bl) (r il) d -> bh (bl r) (il d)", bh=BH, il=IL)
+    z_rows = z.rearrange(
+        "(bh bl) (r il) (jq t) d -> bh il jq (bl r) (t d)", bh=BH, il=IL, t=PACK
+    )
+    xj_rows = xj_p.rearrange("(bh bl) (jq t) k -> bh jq bl (t k)", bh=BH, t=PACK)
+    mask_rows = node_mask.rearrange("(bh bl) j -> bl bh j", bh=BH)
+
+    def where(c):
+        bh, rest = divmod(c, JQ * IL)
+        jq, il = divmod(rest, IL)
+        return bh, jq, il
+
+    with ExitStack() as ctx:
+        ctx.enter_context(tc.manual_schedule())
+        const = ctx.enter_context(tc.tile_pool(name="const", bufs=1))
+        loads = ctx.enter_context(tc.tile_pool(name="loads", bufs=3))
+        work = ctx.enter_context(tc.tile_pool(name="work", bufs=2))
+        psum = ctx.enter_context(tc.psum_pool(name="psum", bufs=1))
+
+        mb1_all = const.tile([P, HID], BF16)
+        xi_sb = const.tile([P, BH, IL, HID], BF16)
+        g_sb = const.tile([P, BH, IL, D_OUT], BF16)
+        mask_bf = const.tile([P, BH, NODES], BF16)
+        mask_f32 = const.tile([P, BH, NODES], F32)
+        recv = const.tile([P, BH, IL, HID], F32)
+        acc = [psum.tile([P, D_OUT], F32, name="acc%d" % kt) for kt in range(K_TILES)]
+        send, z_sb, g_mask, h_bf, dz_bf = {}, {}, {}, {}, {}
+
+        def load_half(bh):
+            nc.sync.dma_start(
+                out=xi_sb[:, bh, :, :].rearrange("p il k -> p (il k)"), in_=xi_rows[bh]
+            )
+            nc.sync.dma_start(
+                out=g_sb[:, bh, :, :].rearrange("p il d -> p (il d)"), in_=g_rows[bh]
+            )
+
+        def add_bias(bh):
+            nc.vector.tensor_tensor(
+                out=recv[:, bh, :, :],
+                in0=xi_sb[:, bh, :, :],
+                in1=mb1_all[:].unsqueeze(1).to_broadcast([P, IL, HID]),
+                op=ALU.add,
+            )
+
+        def load_pass(c):
+            bh, jq, il = where(c)
+            if il == 0:
+                send[c // IL] = loads.tile([P, PACK, HID], BF16, name="send")
+                for r in range(R):
+                    nc.sync.dma_start(
+                        out=send[c // IL][r:P:R, :, :].rearrange("p t k -> p (t k)"),
+                        in_=xj_rows[bh, jq],
+                    )
+            z_sb[c] = loads.tile([P, PACK, D_OUT], F32, name="z_sb")
+            nc.sync.dma_start(
+                out=z_sb[c][:].rearrange("p t d -> p (t d)"), in_=z_rows[bh, il, jq]
+            )
+
+        def mask_grad(c):
+            bh, jq, il = where(c)
+            g_mask[c] = work.tile([P, PACK, D_OUT], BF16, name="g_mask")
+            for t in range(PACK):
+                j = PACK * jq + t
+                nc.scalar.activation(
+                    out=g_mask[c][:, t, :],
+                    in_=g_sb[:, bh, il, :],
+                    func=ACT.Copy,
+                    scale=mask_f32[:, bh, j : j + 1],
+                )
+
+        def make_dz(c):
+            dz_bf[c] = work.tile([P, D_OUT, PACK], BF16, name="dz_bf", align_bytes=64)
+            nc.vector.scalar_tensor_tensor(
+                out=dz_bf[c][:],
+                in0=z_sb[c][:].rearrange("p t d -> p d t"),
+                scalar=0.0,
+                in1=g_mask[c][:].rearrange("p t d -> p d t"),
+                op0=ALU.is_gt,
+                op1=ALU.mult,
+            )
+
+        def make_h(c):
+            bh, jq, il = where(c)
+            for half in range(H_HALVES):
+                cols = slice(half * HALF, (half + 1) * HALF)
+                h_sum = work.tile([P, HALF, PACK], BF16, name="h_sum")
+                nc.vector.tensor_tensor(
+                    out=h_sum[:],
+                    in0=recv[:, bh, il, cols].unsqueeze(2).to_broadcast([P, HALF, PACK]),
+                    in1=send[c // IL][:, :, cols].rearrange("p t k -> p k t"),
+                    op=ALU.add,
+                )
+                h_bf[c, half] = work.tile([P, HALF * PACK], BF16, name="h_bf%d" % half, align_bytes=64)
+                nc.scalar.activation(
+                    out=h_bf[c, half][:],
+                    in_=h_sum[:].rearrange("p k t -> p (k t)"),
+                    func=ACT.Relu,
+                )
+
+        def multiply(c):
+            dz_codes = work.tile([P, D_OUT], U32, name="dz_codes", align_bytes=64)
+            dz_scales = work.tile([P, D_OUT], U8, name="dz_scales", align_bytes=64)
+            nc.vector.quantize_mx(
+                out=dz_codes[:].bitcast(E5M2_X4),
+                scales=dz_scales[:],
+                in_=dz_bf[c][:].rearrange("p d t -> p (d t)"),
+            )
+            for half in range(H_HALVES):
+                h_codes = work.tile([P, HALF], U32, name="h_codes", align_bytes=64)
+                h_scales = work.tile([P, HALF], U8, name="h_scales", align_bytes=64)
+                nc.vector.quantize_mx(
+                    out=h_codes[:].bitcast(E4M3_X4), scales=h_scales[:], in_=h_bf[c, half][:]
+                )
+                for m in range(HALF // P):
+                    cols = slice(m * P, (m + 1) * P)
+                    nc.tensor.matmul_mx(
+                        out=acc[half * (HALF // P) + m][:],
+                        lhsT=h_codes[:, cols].bitcast(E4M3_X4),
+                        lhsT_scale=h_scales[:, cols],
+                        rhs=dz_codes[:].bitcast(E5M2_X4),
+                        rhs_scale=dz_scales[:],
+                        start=(c == 0),
+                        stop=(c == N_PASS - 1),
+                    )
+
+        nc.sync.dma_start(out=mb1_all[:], in_=mb1.partition_broadcast(P))
+        load_half(0)
+        for r in range(R):
+            nc.sync.dma_start(out=mask_bf[r:P:R, :, :], in_=mask_rows)
+        load_pass(0)
+        load_pass(1)
+        nc.vector.tensor_copy(out=mask_f32[:], in_=mask_bf[:])
+        add_bias(0)
+        mask_grad(0)
+
+        for c in range(N_PASS + 1):
+            if c + 2 < N_PASS:
+                load_pass(c + 2)
+            if c == 0:
+                load_half(1)
+            if c + 1 < N_PASS:
+                mask_grad(c + 1)
+            if c < N_PASS:
+                make_dz(c)
+                make_h(c)
+            if c + 2 == JQ * IL:
+                add_bias(1)
+            if c > 0:
+                multiply(c - 1)
+
+        for kt in range(K_TILES):
+            res = loads.tile([P, D_OUT], F32, name="res")
+            if kt % 2 == 0:
+                nc.scalar.copy(out=res[:], in_=acc[kt][:])
+            else:
+                nc.vector.tensor_copy(out=res[:], in_=acc[kt][:])
+            nc.sync.dma_start(out=out[kt * P : (kt + 1) * P, :], in_=res[:])

@@ -35,6 +35,7 @@ BYTES = (
 H_HALVES = 2
 HALF = HID // H_HALVES
 N_PASS = BH * JQ * IL
+RUN = 4
 
 
 def tile_graphdynamics_pa_t_v_kernel(
@@ -130,9 +131,12 @@ def tile_graphdynamics_pa_t_v_kernel(
                 cols = slice(half * HALF, (half + 1) * HALF)
                 h_sum = work.tile([P, HALF, PACK], BF16, name="h_sum")
                 nc.vector.tensor_tensor(
-                    out=h_sum[:],
-                    in0=recv[:, bh, il, cols].unsqueeze(2).to_broadcast([P, HALF, PACK]),
-                    in1=send[c // IL][:, :, cols].rearrange("p t k -> p k t"),
+                    out=h_sum[:].rearrange("p (n i) t -> p n t i", i=RUN),
+                    in0=recv[:, bh, il, cols]
+                    .rearrange("p (n i) -> p n i", i=RUN)
+                    .unsqueeze(2)
+                    .to_broadcast([P, HALF // RUN, PACK, RUN]),
+                    in1=send[c // IL][:, :, cols].rearrange("p t (n i) -> p n t i", i=RUN),
                     op=ALU.add,
                 )
                 h_bf[c, half] = work.tile([P, HALF * PACK], BF16, name="h_bf%d" % half, align_bytes=64)

@@ -32,8 +32,6 @@ BYTES = (
 )
 
 
-H_HALVES = 2
-HALF = HID // H_HALVES
 N_PASS = BH * JQ * IL
 RUN = 4
 
@@ -51,11 +49,6 @@ def tile_graphdynamics_pa_t_v_kernel(
     xj_rows = xj_p.rearrange("(bh bl) (jq t) k -> bh jq bl (t k)", bh=BH, t=PACK)
     mask_rows = node_mask.rearrange("(bh bl) j -> bl bh j", bh=BH)
 
-    def where(c):
-        bh, rest = divmod(c, JQ * IL)
-        jq, il = divmod(rest, IL)
-        return bh, jq, il
-
     with ExitStack() as ctx:
         ctx.enter_context(tc.manual_schedule())
         const = ctx.enter_context(tc.tile_pool(name="const", bufs=1))
@@ -70,12 +63,14 @@ def tile_graphdynamics_pa_t_v_kernel(
         mask_f32 = const.tile([P, BH, NODES], F32)
         recv = const.tile([P, BH, IL, HID], F32)
         acc = [psum.tile([P, D_OUT], F32, name="acc%d" % kt) for kt in range(K_TILES)]
-        send, z_sb, g_mask, h_bf, dz_bf = {}, {}, {}, {}, {}
+        send, g_mask, z_sb, h_bf, dz_bf = {}, {}, {}, {}, {}
 
-        def load_half(bh):
+        def load_xi(bh):
             nc.sync.dma_start(
                 out=xi_sb[:, bh, :, :].rearrange("p il k -> p (il k)"), in_=xi_rows[bh]
             )
+
+        def load_g(bh):
             nc.sync.dma_start(
                 out=g_sb[:, bh, :, :].rearrange("p il d -> p (il d)"), in_=g_rows[bh]
             )
@@ -88,63 +83,63 @@ def tile_graphdynamics_pa_t_v_kernel(
                 op=ALU.add,
             )
 
-        def load_pass(c):
-            bh, jq, il = where(c)
-            if il == 0:
-                send[c // IL] = loads.tile([P, PACK, HID], BF16, name="send")
-                for r in range(R):
-                    nc.sync.dma_start(
-                        out=send[c // IL][r:P:R, :, :].rearrange("p t k -> p (t k)"),
-                        in_=xj_rows[bh, jq],
-                    )
+        def load_send(q):
+            bh, jq = divmod(q, JQ)
+            send[q] = loads.tile([P, PACK, HID], BF16, name="send")
+            for r in range(R):
+                nc.sync.dma_start(
+                    out=send[q][r:P:R, :, :].rearrange("p t k -> p (t k)"), in_=xj_rows[bh, jq]
+                )
+
+        def load_z(c):
+            q, il = divmod(c, IL)
+            bh, jq = divmod(q, JQ)
             z_sb[c] = loads.tile([P, PACK, D_OUT], F32, name="z_sb")
             nc.sync.dma_start(
                 out=z_sb[c][:].rearrange("p t d -> p (t d)"), in_=z_rows[bh, il, jq]
             )
 
-        def mask_grad(c):
-            bh, jq, il = where(c)
-            g_mask[c] = work.tile([P, PACK, D_OUT], BF16, name="g_mask")
+        def mask_grad(q):
+            bh, jq = divmod(q, JQ)
+            g_mask[q] = work.tile([P, IL, PACK, D_OUT], BF16, name="g_mask")
             for t in range(PACK):
                 j = PACK * jq + t
                 nc.scalar.activation(
-                    out=g_mask[c][:, t, :],
-                    in_=g_sb[:, bh, il, :],
+                    out=g_mask[q][:, :, t, :],
+                    in_=g_sb[:, bh, :, :],
                     func=ACT.Copy,
                     scale=mask_f32[:, bh, j : j + 1],
                 )
 
+        def make_h(c):
+            q, il = divmod(c, IL)
+            bh = q // JQ
+            h_sum = work.tile([P, HID, PACK], BF16, name="h_sum")
+            nc.vector.tensor_tensor(
+                out=h_sum[:].rearrange("p (n i) t -> p n t i", i=RUN),
+                in0=recv[:, bh, il, :]
+                .rearrange("p (n i) -> p n i", i=RUN)
+                .unsqueeze(2)
+                .to_broadcast([P, HID // RUN, PACK, RUN]),
+                in1=send[q][:].rearrange("p t (n i) -> p n t i", i=RUN),
+                op=ALU.add,
+            )
+            h_bf[c] = work.tile([P, HID * PACK], BF16, name="h_bf", align_bytes=64)
+            nc.scalar.activation(
+                out=h_bf[c][:], in_=h_sum[:].rearrange("p k t -> p (k t)"), func=ACT.Relu
+            )
+
         def make_dz(c):
+            q, il = divmod(c, IL)
             dz_bf[c] = work.tile([P, D_OUT, PACK], BF16, name="dz_bf", align_bytes=64)
             nc.vector.scalar_tensor_tensor(
                 out=dz_bf[c][:],
                 in0=z_sb[c][:].rearrange("p t d -> p d t"),
                 scalar=0.0,
-                in1=g_mask[c][:].rearrange("p t d -> p d t"),
+                in1=g_mask[q][:, il, :, :].rearrange("p t d -> p d t"),
                 op0=ALU.is_gt,
                 op1=ALU.mult,
             )
-
-        def make_h(c):
-            bh, jq, il = where(c)
-            for half in range(H_HALVES):
-                cols = slice(half * HALF, (half + 1) * HALF)
-                h_sum = work.tile([P, HALF, PACK], BF16, name="h_sum")
-                nc.vector.tensor_tensor(
-                    out=h_sum[:].rearrange("p (n i) t -> p n t i", i=RUN),
-                    in0=recv[:, bh, il, cols]
-                    .rearrange("p (n i) -> p n i", i=RUN)
-                    .unsqueeze(2)
-                    .to_broadcast([P, HALF // RUN, PACK, RUN]),
-                    in1=send[c // IL][:, :, cols].rearrange("p t (n i) -> p n t i", i=RUN),
-                    op=ALU.add,
-                )
-                h_bf[c, half] = work.tile([P, HALF * PACK], BF16, name="h_bf%d" % half, align_bytes=64)
-                nc.scalar.activation(
-                    out=h_bf[c, half][:],
-                    in_=h_sum[:].rearrange("p k t -> p (k t)"),
-                    func=ACT.Relu,
-                )
 
         def multiply(c):
             dz_codes = work.tile([P, D_OUT], U32, name="dz_codes", align_bytes=64)
@@ -154,44 +149,48 @@ def tile_graphdynamics_pa_t_v_kernel(
                 scales=dz_scales[:],
                 in_=dz_bf[c][:].rearrange("p d t -> p (d t)"),
             )
-            for half in range(H_HALVES):
-                h_codes = work.tile([P, HALF], U32, name="h_codes", align_bytes=64)
-                h_scales = work.tile([P, HALF], U8, name="h_scales", align_bytes=64)
-                nc.vector.quantize_mx(
-                    out=h_codes[:].bitcast(E4M3_X4), scales=h_scales[:], in_=h_bf[c, half][:]
+            h_codes = work.tile([P, HID], U32, name="h_codes", align_bytes=64)
+            h_scales = work.tile([P, HID], U8, name="h_scales", align_bytes=64)
+            nc.vector.quantize_mx(
+                out=h_codes[:].bitcast(E4M3_X4), scales=h_scales[:], in_=h_bf[c][:]
+            )
+            for kt in range(K_TILES):
+                cols = slice(kt * P, (kt + 1) * P)
+                nc.tensor.matmul_mx(
+                    out=acc[kt][:],
+                    lhsT=h_codes[:, cols].bitcast(E4M3_X4),
+                    lhsT_scale=h_scales[:, cols],
+                    rhs=dz_codes[:].bitcast(E5M2_X4),
+                    rhs_scale=dz_scales[:],
+                    start=(c == 0),
+                    stop=(c == N_PASS - 1),
                 )
-                for m in range(HALF // P):
-                    cols = slice(m * P, (m + 1) * P)
-                    nc.tensor.matmul_mx(
-                        out=acc[half * (HALF // P) + m][:],
-                        lhsT=h_codes[:, cols].bitcast(E4M3_X4),
-                        lhsT_scale=h_scales[:, cols],
-                        rhs=dz_codes[:].bitcast(E5M2_X4),
-                        rhs_scale=dz_scales[:],
-                        start=(c == 0),
-                        stop=(c == N_PASS - 1),
-                    )
 
+        load_xi(0)
         nc.sync.dma_start(out=mb1_all[:], in_=mb1.partition_broadcast(P))
-        load_half(0)
+        load_send(0)
         for r in range(R):
             nc.sync.dma_start(out=mask_bf[r:P:R, :, :], in_=mask_rows)
-        load_pass(0)
-        load_pass(1)
-        nc.vector.tensor_copy(out=mask_f32[:], in_=mask_bf[:])
+        load_g(0)
+        load_z(0)
+        load_z(1)
         add_bias(0)
+        nc.scalar.copy(out=mask_f32[:], in_=mask_bf[:])
         mask_grad(0)
 
         for c in range(N_PASS + 1):
             if c + 2 < N_PASS:
-                load_pass(c + 2)
+                if (c + 2) % IL == 0:
+                    load_send((c + 2) // IL)
+                load_z(c + 2)
             if c == 0:
-                load_half(1)
-            if c + 1 < N_PASS:
-                mask_grad(c + 1)
+                load_xi(1)
+                load_g(1)
             if c < N_PASS:
-                make_dz(c)
                 make_h(c)
+                if c % IL == 0 and c // IL + 1 < BH * JQ:
+                    mask_grad(c // IL + 1)
+                make_dz(c)
             if c + 2 == JQ * IL:
                 add_bias(1)
             if c > 0:

@@ -63,7 +63,7 @@ def tile_graphdynamics_pa_t_v_kernel(
         mask_f32 = const.tile([P, BH, NODES], F32)
         recv = const.tile([P, BH, IL, HID], F32)
         acc = [psum.tile([P, D_OUT], F32, name="acc%d" % kt) for kt in range(K_TILES)]
-        send, g_mask, z_sb, h_bf, dz_bf = {}, {}, {}, {}, {}
+        send, g_mask, z_sb, h_bf, dz_rows, dz_bf, dz_codes, dz_scales = {}, {}, {}, {}, {}, {}, {}, {}
 
         def load_xi(bh):
             nc.sync.dma_start(
@@ -131,24 +131,33 @@ def tile_graphdynamics_pa_t_v_kernel(
 
         def make_dz(c):
             q, il = divmod(c, IL)
-            dz_bf[c] = work.tile([P, D_OUT, PACK], BF16, name="dz_bf", align_bytes=64)
+            dz_rows[c] = work.tile([P, PACK, D_OUT], BF16, name="dz_rows")
             nc.vector.scalar_tensor_tensor(
-                out=dz_bf[c][:],
-                in0=z_sb[c][:].rearrange("p t d -> p d t"),
+                out=dz_rows[c][:].rearrange("p t d -> p (t d)"),
+                in0=z_sb[c][:].rearrange("p t d -> p (t d)"),
                 scalar=0.0,
-                in1=g_mask[q][:, il, :, :].rearrange("p t d -> p d t"),
+                in1=g_mask[q][:, il, :, :].rearrange("p t d -> p (t d)"),
                 op0=ALU.is_gt,
                 op1=ALU.mult,
             )
 
-        def multiply(c):
-            dz_codes = work.tile([P, D_OUT], U32, name="dz_codes", align_bytes=64)
-            dz_scales = work.tile([P, D_OUT], U8, name="dz_scales", align_bytes=64)
+        def regroup_dz(c):
+            dz_bf[c] = work.tile([P, D_OUT, PACK], BF16, name="dz_bf", align_bytes=64)
+            nc.vector.tensor_copy(
+                out=dz_bf[c][:].rearrange("p (n i) t -> p n t i", i=RUN),
+                in_=dz_rows[c][:].rearrange("p t (n i) -> p n t i", i=RUN),
+            )
+
+        def quantise_dz(c):
+            dz_codes[c] = work.tile([P, D_OUT], U32, name="dz_codes", align_bytes=64)
+            dz_scales[c] = work.tile([P, D_OUT], U8, name="dz_scales", align_bytes=64)
             nc.vector.quantize_mx(
-                out=dz_codes[:].bitcast(E5M2_X4),
-                scales=dz_scales[:],
+                out=dz_codes[c][:].bitcast(E5M2_X4),
+                scales=dz_scales[c][:],
                 in_=dz_bf[c][:].rearrange("p d t -> p (d t)"),
             )
+
+        def multiply(c):
             h_codes = work.tile([P, HID], U32, name="h_codes", align_bytes=64)
             h_scales = work.tile([P, HID], U8, name="h_scales", align_bytes=64)
             nc.vector.quantize_mx(
@@ -160,8 +169,8 @@ def tile_graphdynamics_pa_t_v_kernel(
                     out=acc[kt][:],
                     lhsT=h_codes[:, cols].bitcast(E4M3_X4),
                     lhsT_scale=h_scales[:, cols],
-                    rhs=dz_codes[:].bitcast(E5M2_X4),
-                    rhs_scale=dz_scales[:],
+                    rhs=dz_codes[c][:].bitcast(E5M2_X4),
+                    rhs_scale=dz_scales[c][:],
                     start=(c == 0),
                     stop=(c == N_PASS - 1),
                 )
@@ -193,6 +202,10 @@ def tile_graphdynamics_pa_t_v_kernel(
                 make_dz(c)
             if c + 2 == JQ * IL:
                 add_bias(1)
+            if c > 0:
+                quantise_dz(c - 1)
+            if c < N_PASS:
+                regroup_dz(c)
             if c > 0:
                 multiply(c - 1)
 

from contextlib import ExitStack

import concourse.mybir as mybir

F32 = mybir.dt.float32
BF16 = mybir.dt.bfloat16
U32 = mybir.dt.uint32
U8 = mybir.dt.uint8
E4M3_X4 = mybir.dt.float8_e4m3fn_x4
E5M2_X4 = mybir.dt.float8_e5m2_x4
ALU = mybir.AluOpType
ACT = mybir.ActivationFunctionType

P = 128
PACK = 4
GRAPHS, NODES, D_OUT, HID = 32, 16, 512, 1024
BH = 2
BL = GRAPHS // BH
R = P // BL
IL = NODES // R
JQ = NODES // PACK
K_TILES = HID // P

FLOPS = 2 * GRAPHS * NODES * NODES * HID * D_OUT
BYTES = (
    GRAPHS * NODES * NODES * D_OUT * 4
    + 2 * GRAPHS * NODES * HID * 2
    + GRAPHS * NODES * D_OUT * 2
    + GRAPHS * NODES * 2
    + HID * 2
    + HID * D_OUT * 4
)


N_PASS = BH * JQ * IL
RUN = 4


def tile_graphdynamics_pa_t_v_kernel(
    tc, xi_p, xj_p, node_mask, mb1, mw2, mb2, z, grad_out, out
):
    nc = tc.nc

    xi_rows = xi_p.rearrange("(bh bl) (r il) k -> bh (bl r) (il k)", bh=BH, il=IL)
    g_rows = grad_out.rearrange("(bh bl) (r il) d -> bh (bl r) (il d)", bh=BH, il=IL)
    z_rows = z.rearrange(
        "(bh bl) (r il) (jq t) d -> bh il jq (bl r) (t d)", bh=BH, il=IL, t=PACK
    )
    xj_rows = xj_p.rearrange("(bh bl) (jq t) k -> bh jq bl (t k)", bh=BH, t=PACK)
    mask_rows = node_mask.rearrange("(bh bl) j -> bl bh j", bh=BH)

    with ExitStack() as ctx:
        ctx.enter_context(tc.manual_schedule())
        const = ctx.enter_context(tc.tile_pool(name="const", bufs=1))
        loads = ctx.enter_context(tc.tile_pool(name="loads", bufs=3))
        work = ctx.enter_context(tc.tile_pool(name="work", bufs=2))
        psum = ctx.enter_context(tc.psum_pool(name="psum", bufs=1))

        mb1_all = const.tile([P, HID], BF16)
        xi_sb = const.tile([P, BH, IL, HID], BF16)
        g_sb = const.tile([P, BH, IL, D_OUT], BF16)
        mask_bf = const.tile([P, BH, NODES], BF16)
        mask_f32 = const.tile([P, BH, NODES], F32)
        recv = const.tile([P, BH, IL, HID], F32)
        acc = [psum.tile([P, D_OUT], F32, name="acc%d" % kt) for kt in range(K_TILES)]
        send, g_mask, z_sb, h_bf, dz_rows, dz_bf, dz_codes, dz_scales = {}, {}, {}, {}, {}, {}, {}, {}

        def load_xi(bh):
            nc.sync.dma_start(
                out=xi_sb[:, bh, :, :].rearrange("p il k -> p (il k)"), in_=xi_rows[bh]
            )

        def load_g(bh):
            nc.sync.dma_start(
                out=g_sb[:, bh, :, :].rearrange("p il d -> p (il d)"), in_=g_rows[bh]
            )

        def add_bias(bh):
            nc.vector.tensor_tensor(
                out=recv[:, bh, :, :],
                in0=xi_sb[:, bh, :, :],
                in1=mb1_all[:].unsqueeze(1).to_broadcast([P, IL, HID]),
                op=ALU.add,
            )

        def load_send(q):
            bh, jq = divmod(q, JQ)
            send[q] = loads.tile([P, PACK, HID], BF16, name="send")
            for r in range(R):
                nc.sync.dma_start(
                    out=send[q][r:P:R, :, :].rearrange("p t k -> p (t k)"), in_=xj_rows[bh, jq]
                )

        def load_z(c):
            q, il = divmod(c, IL)
            bh, jq = divmod(q, JQ)
            z_sb[c] = loads.tile([P, PACK, D_OUT], F32, name="z_sb")
            nc.sync.dma_start(
                out=z_sb[c][:].rearrange("p t d -> p (t d)"), in_=z_rows[bh, il, jq]
            )

        def mask_grad(q):
            bh, jq = divmod(q, JQ)
            g_mask[q] = work.tile([P, IL, PACK, D_OUT], BF16, name="g_mask")
            for t in range(PACK):
                j = PACK * jq + t
                nc.scalar.activation(
                    out=g_mask[q][:, :, t, :],
                    in_=g_sb[:, bh, :, :],
                    func=ACT.Copy,
                    scale=mask_f32[:, bh, j : j + 1],
                )

        def make_h(c):
            q, il = divmod(c, IL)
            bh = q // JQ
            h_sum = work.tile([P, HID, PACK], BF16, name="h_sum")
            nc.vector.tensor_tensor(
                out=h_sum[:].rearrange("p (n i) t -> p n t i", i=RUN),
                in0=recv[:, bh, il, :]
                .rearrange("p (n i) -> p n i", i=RUN)
                .unsqueeze(2)
                .to_broadcast([P, HID // RUN, PACK, RUN]),
                in1=send[q][:].rearrange("p t (n i) -> p n t i", i=RUN),
                op=ALU.add,
            )
            h_bf[c] = work.tile([P, HID * PACK], BF16, name="h_bf", align_bytes=64)
            nc.scalar.activation(
                out=h_bf[c][:], in_=h_sum[:].rearrange("p k t -> p (k t)"), func=ACT.Relu
            )

        def make_dz(c):
            q, il = divmod(c, IL)
            dz_rows[c] = work.tile([P, PACK, D_OUT], BF16, name="dz_rows")
            nc.vector.scalar_tensor_tensor(
                out=dz_rows[c][:].rearrange("p t d -> p (t d)"),
                in0=z_sb[c][:].rearrange("p t d -> p (t d)"),
                scalar=0.0,
                in1=g_mask[q][:, il, :, :].rearrange("p t d -> p (t d)"),
                op0=ALU.is_gt,
                op1=ALU.mult,
            )

        def regroup_dz(c):
            dz_bf[c] = work.tile([P, D_OUT, PACK], BF16, name="dz_bf", align_bytes=64)
            nc.vector.tensor_copy(
                out=dz_bf[c][:].rearrange("p (n i) t -> p n t i", i=RUN),
                in_=dz_rows[c][:].rearrange("p t (n i) -> p n t i", i=RUN),
            )

        def quantise_dz(c):
            dz_codes[c] = work.tile([P, D_OUT], U32, name="dz_codes", align_bytes=64)
            dz_scales[c] = work.tile([P, D_OUT], U8, name="dz_scales", align_bytes=64)
            nc.vector.quantize_mx(
                out=dz_codes[c][:].bitcast(E5M2_X4),
                scales=dz_scales[c][:],
                in_=dz_bf[c][:].rearrange("p d t -> p (d t)"),
            )

        def multiply(c):
            h_codes = work.tile([P, HID], U32, name="h_codes", align_bytes=64)
            h_scales = work.tile([P, HID], U8, name="h_scales", align_bytes=64)
            nc.vector.quantize_mx(
                out=h_codes[:].bitcast(E4M3_X4), scales=h_scales[:], in_=h_bf[c][:]
            )
            for kt in range(K_TILES):
                cols = slice(kt * P, (kt + 1) * P)
                nc.tensor.matmul_mx(
                    out=acc[kt][:],
                    lhsT=h_codes[:, cols].bitcast(E4M3_X4),
                    lhsT_scale=h_scales[:, cols],
                    rhs=dz_codes[c][:].bitcast(E5M2_X4),
                    rhs_scale=dz_scales[c][:],
                    start=(c == 0),
                    stop=(c == N_PASS - 1),
                )

        load_xi(0)
        nc.sync.dma_start(out=mb1_all[:], in_=mb1.partition_broadcast(P))
        load_send(0)
        for r in range(R):
            nc.sync.dma_start(out=mask_bf[r:P:R, :, :], in_=mask_rows)
        load_g(0)
        load_z(0)
        load_z(1)
        add_bias(0)
        nc.scalar.copy(out=mask_f32[:], in_=mask_bf[:])
        mask_grad(0)

        for c in range(N_PASS + 1):
            if c + 2 < N_PASS:
                if (c + 2) % IL == 0:
                    load_send((c + 2) // IL)
                load_z(c + 2)
            if c == 0:
                load_xi(1)
                load_g(1)
            if c < N_PASS:
                make_h(c)
                if c % IL == 0 and c // IL + 1 < BH * JQ:
                    mask_grad(c // IL + 1)
                make_dz(c)
            if c + 2 == JQ * IL:
                add_bias(1)
            if c > 0:
                quantise_dz(c - 1)
            if c < N_PASS:
                regroup_dz(c)
            if c > 0:
                multiply(c - 1)

        for kt in range(K_TILES):
            res = loads.tile([P, D_OUT], F32, name="res")
            if kt % 2 == 0:
                nc.scalar.copy(out=res[:], in_=acc[kt][:])
            else:
                nc.vector.tensor_copy(out=res[:], in_=acc[kt][:])
            nc.sync.dma_start(out=out[kt * P : (kt + 1) * P, :], in_=res[:])
